import numpy as np
import ml_dtypes


def mxq(x, axis, fmt="e4m3"):
    dtype, down = {"e4m3": (ml_dtypes.float8_e4m3fn, 7), "e5m2": (ml_dtypes.float8_e5m2, 14)}[fmt]
    v = np.moveaxis(np.asarray(x, np.float32).astype(ml_dtypes.bfloat16).astype(np.float64), axis, -1)
    blocks = v.reshape(v.shape[:-1] + (-1, 32))
    amax = np.abs(blocks).max(-1, keepdims=True)
    byte = np.maximum(np.where(amax > 0, np.frexp(amax)[1] - 1 + 127, 0) - down, 1)
    scale = np.exp2(byte - 127.0)
    codes = (blocks / scale).astype(np.float32).astype(dtype).astype(np.float64)
    return np.moveaxis((codes * scale).reshape(v.shape), -1, axis)


WIDE = False


def mx_kscale(k):
    if not WIDE:
        return np.ones(k)
    levels = np.array([10, -10, 5, -5, 0])
    a = np.random.permutation(np.resize(levels, k // 512 * 4)).reshape(k // 512, 4)
    idx = np.arange(k)
    return np.exp2(a[idx // 512, idx % 128 // 32])


BF16 = ml_dtypes.bfloat16


def bf(x):
    return np.asarray(x, np.float32).astype(BF16)


def f64(x):
    return np.asarray(x).astype(np.float64)


LAG_IDXS = list(range(-10, 41))
B, T = 2, 512
IN_DIM = 512
OUT_DIM = 128
REAL_IN_DIM = len(LAG_IDXS) * IN_DIM


def time_lagging(x):
    nb, nt, nd = x.shape
    parts = []
    for lag in LAG_IDXS:
        if lag > 0:
            s = np.pad(x[:, : nt - lag], ((0, 0), (lag, 0), (0, 0)))
        elif lag < 0:
            s = np.pad(x[:, -lag:], ((0, 0), (0, -lag), (0, 0)))
        else:
            s = x
        parts.append(s)
    return np.concatenate(parts, axis=-1)


def setup_inputs():
    s = mx_kscale(IN_DIM)
    sk = np.tile(s, len(LAG_IDXS))
    return {"x": bf(np.random.standard_normal((B, T, IN_DIM)) * s),
            "W": bf(np.random.standard_normal((OUT_DIM, REAL_IN_DIM)) * (REAL_IN_DIM ** -0.5) / sk[None, :]),
            "b": bf(np.random.standard_normal(OUT_DIM) * 0.3)}


def reference(x, W, b):
    lagged = time_lagging(f64(x))
    return (mxq(lagged, 2, "e4m3") @ mxq(f64(W), 1, "e4m3").T) + f64(b)

@@ -1,0 +1,269 @@
+from contextlib import ExitStack
+
+import concourse.mybir as mybir
+from concourse.masks import make_identity
+
+F32 = mybir.dt.float32
+BF16 = mybir.dt.bfloat16
+U32 = mybir.dt.uint32
+U8 = mybir.dt.uint8
+I32 = mybir.dt.int32
+FP8X4 = mybir.dt.float8_e4m3fn_x4
+
+P = 128
+N_LAGS = 51
+D = 512
+T = 512
+NB = 2
+O = 128
+WORDS = D // 2
+
+Q = 16
+R = 32
+BASE = 40
+N_BLK = R + N_LAGS - 1
+XCOLS = N_BLK * Q
+
+ROUNDS = (2, 2, 4, 8, 12, 12, 11)
+N_BANKS = 6
+TAIL_ROUNDS = 2
+
+FLOPS = 2 * NB * T * N_LAGS * D * O
+
+
+def tile_ctrf_kernel(tc, x, W, b, out):
+    nc = tc.nc
+    n_rounds = len(ROUNDS)
+    first_lag = [sum(ROUNDS[:r]) for r in range(n_rounds)]
+    first_unit = [4 + sum([(n + 1) // 2 for n in ROUNDS[:r]]) for r in range(n_rounds)]
+    epi_unit = 4 + sum([(n + 1) // 2 for n in ROUNDS])
+    lag_round = []
+    for r in range(n_rounds):
+        lag_round.extend([r] * ROUNDS[r])
+
+    with ExitStack() as ctx:
+        keep = ctx.enter_context(tc.tile_pool(name="keep", bufs=1))
+        accp = ctx.enter_context(tc.psum_pool(name="accp", bufs=1))
+        tpp = ctx.enter_context(tc.psum_pool(name="tpp", bufs=1))
+        ctx.enter_context(tc.manual_schedule())
+
+        x_rows = x.rearrange("n t d -> (n t) d")
+        x_raw = []
+        for h in range(4):
+            xr = keep.tile([P, 2, D], BF16, name="x_raw%d" % h)
+            nc.sync.dma_start(
+                out=xr[:],
+                in_=x_rows[h * 256 : (h + 1) * 256, :].rearrange("(j p) d -> p j d", p=P),
+            )
+            x_raw.append(xr)
+        w_raw = []
+        for r in range(n_rounds):
+            wr = keep.tile([P, ROUNDS[r] * D], BF16, name="w_raw%d" % r)
+            nc.sync.dma_start(
+                out=wr[:], in_=W[:, first_lag[r] * D : (first_lag[r] + ROUNDS[r]) * D]
+            )
+            w_raw.append(wr)
+
+        xe = []
+        xq = []
+        xs = []
+        for n in range(NB):
+            e = keep.tile([P, XCOLS * 4], BF16, name="xe%d" % n, align_bytes=64)
+            ei = e[:].bitcast(I32).rearrange("p (r q u) -> p r q u", q=Q, u=2)
+            nc.vector.memset(ei[:, 0:BASE, 0:2, :], 0)
+            nc.vector.memset(ei[:, BASE + R : N_BLK, Q - 1 : Q, :], 0)
+            xe.append(e)
+            xq.append(keep.tile([P, XCOLS], U32, name="xq%d" % n, align_bytes=64))
+            planes = []
+            for j in range(4):
+                planes.append(keep.tile([P, XCOLS], U8, name="xs%d_%d" % (n, j), align_bytes=64))
+            nc.vector.memset(planes[0][:].bitcast(I32), 0)
+            xs.append(planes)
+        ident = keep.tile([P, P], F32, name="ident")
+        make_identity(nc, ident[:])
+        bz = keep.tile([P, P], BF16, name="bz")
+        nc.vector.memset(bz[:], 0.0)
+        nc.scalar.dma_start(out=bz[0:1, :], in_=b.rearrange("(a o) -> a o", a=1))
+        bzf = keep.tile([P, P], F32, name="bzf")
+        bias = keep.tile([P, 1], F32, name="bias")
+
+        acc = []
+        for n in range(NB):
+            acc.append(accp.tile([P, T], F32, name="acc%d" % n))
+
+        def bank(unit, shape):
+            return tpp.tile(shape, F32, name="tp_u%d" % unit, tag="tp%d" % (unit % N_BANKS))
+
+        for h in range(4):
+            n = h // 2
+            half = h % 2
+            tp = bank(h, [P, 2, 256])
+            xw = x_raw[h][:].bitcast(F32)
+            for j in range(2):
+                for u in range(2):
+                    nc.tensor.transpose(
+                        tp[:, u, j * P : (j + 1) * P], xw[:, j, u * P : (u + 1) * P], ident[:]
+                    )
+            ew = xe[n][:].bitcast(F32).rearrange("p (r q u) -> p r q u", q=Q, u=2)
+            nc.scalar.copy(
+                out=ew[:, BASE : BASE + R, 8 * half : 8 * half + 8, :],
+                in_=tp[:].rearrange("p u (q r) -> p r q u", r=R),
+            )
+
+        def quantise_x(n, c0, width):
+            nc.vector.quantize_mx(
+                out=xq[n][:, c0 : c0 + width].bitcast(FP8X4),
+                scales=xs[n][0][:, c0 : c0 + width],
+                in_=xe[n][:, 4 * c0 : 4 * (c0 + width)],
+            )
+
+        def shift_planes(n, c0, c1):
+            for j in range(1, 4):
+                end = min(c1, XCOLS - Q * j)
+                nc.vector.tensor_copy(
+                    out=xs[n][j][:, c0:end].bitcast(I32),
+                    in_=xs[n][0][:, c0 + Q * j : end + Q * j].bitcast(I32),
+                )
+
+        def stage_a(n):
+            eb = xe[n][:].rearrange("p (r q e) -> p r q e", q=Q, e=4)
+            nc.vector.tensor_copy(
+                out=eb[:, BASE + R : N_BLK, 0 : Q - 1, :], in_=eb[:, BASE : BASE + N_BLK - BASE - R, 1:Q, :]
+            )
+            quantise_x(n, BASE * Q, 512)
+            quantise_x(n, BASE * Q + 512, 128)
+            quantise_x(n, BASE * Q + 640, 32)
+            shift_planes(n, BASE * Q, XCOLS)
+
+        def stage_b(n):
+            eb = xe[n][:].rearrange("p (r q e) -> p r q e", q=Q, e=4)
+            nc.vector.tensor_copy(
+                out=eb[:, BASE - R : BASE, 1:Q, :], in_=eb[:, BASE : BASE + R, 0 : Q - 1, :]
+            )
+            nc.vector.tensor_copy(
+                out=eb[:, 0 : BASE - R, 2:Q, :], in_=eb[:, 2 * R : BASE + R, 0 : Q - 2, :]
+            )
+            quantise_x(n, 0, 512)
+            quantise_x(n, 512, 128)
+            shift_planes(n, 0, BASE * Q)
+
+        wq = {}
+        ws = {}
+
+        def prepare(r):
+            n = ROUNDS[r]
+            ww = w_raw[r][:].bitcast(F32)
+            g = keep.tile([P, n * D], BF16, name="wg%d" % r, align_bytes=64)
+            gw = g[:].bitcast(F32)
+            for i0 in range(0, n, 2):
+                m = min(2, n - i0)
+                unit = first_unit[r] + i0 // 2
+                on_vector = n > 8 and (i0 // 2) % 3 == 2
+                tp = bank(unit, [P, 4, P])
+                for i in range(m):
+                    for u in range(2):
+                        col = (i0 + i) * WORDS + u * P
+                        nc.tensor.transpose(tp[:, 2 * i + u, :], ww[:, col : col + P], ident[:])
+                if m == 1:
+                    nc.tensor.transpose(tp[:, 2, :], bzf[:], ident[:])
+                dst = gw[:, i0 * WORDS : (i0 + m) * WORDS].rearrange("p (i o u) -> p i o u", i=m, u=2)
+                src = tp[:, 0 : 2 * m, :].rearrange("p (i u) o -> p i o u", u=2)
+                if on_vector:
+                    nc.vector.tensor_copy(out=dst, in_=src)
+                else:
+                    nc.scalar.copy(out=dst, in_=src)
+                if m == 1:
+                    assert on_vector
+                    nc.vector.tensor_copy(out=bias[:], in_=tp[:, 2, 0:1])
+            q = keep.tile([P, n * O], U32, name="wq%d" % r, align_bytes=64)
+            s = keep.tile([P, n * O], U8, name="ws%d" % r, align_bytes=64)
+            i0 = 0
+            for m in (8, 4, 2, 1):
+                if n - i0 >= m:
+                    nc.vector.quantize_mx(
+                        out=q[:, i0 * O : (i0 + m) * O].bitcast(FP8X4),
+                        scales=s[:, i0 * O : (i0 + m) * O],
+                        in_=g[:, i0 * D : (i0 + m) * D],
+                    )
+                    i0 += m
+            wq[r] = q
+            ws[r] = s
+
+        def mx_pass(l, n):
+            r = lag_round[l]
+            i = l - first_lag[r]
+            r0 = N_LAGS - 1 - l
+            j = r0 % 4
+            c0 = Q * (r0 - j)
+            nc.tensor.matmul_mx(
+                out=acc[n][:],
+                lhsT=wq[r][:, i * O : (i + 1) * O].bitcast(FP8X4),
+                lhsT_scale=ws[r][:, i * O : (i + 1) * O],
+                rhs=xq[n][:, Q * r0 : Q * r0 + T].bitcast(FP8X4),
+                rhs_scale=xs[n][j][:, c0 : c0 + T],
+                start=(l == 0),
+                stop=(l == N_LAGS - 1),
+            )
+
+        def multiply(r):
+            for n in range(NB):
+                for l in range(first_lag[r], first_lag[r] + ROUNDS[r]):
+                    mx_pass(l, n)
+
+        out_t = {}
+
+        def evacuate(n):
+            o_t = keep.tile([P, T], F32, name="out_t%d" % n)
+            nc.vector.tensor_scalar_add(
+                out=o_t[:].rearrange("p (q r) -> p q r", r=R),
+                in0=acc[n][:].rearrange("p (r q) -> p q r", q=Q),
+                scalar1=bias[:, 0:1],
+            )
+            out_t[n] = o_t
+
+        def finish(n):
+            for half in range(2):
+                unit = epi_unit + 2 * n + half
+                tp = bank(unit, [P, 4, P])
+                for j in range(2):
+                    t0 = (2 * half + j) * P
+                    nc.tensor.transpose(tp[:, j, :], out_t[n][:, t0 : t0 + P], ident[:])
+                res = keep.tile([P, 2, O], F32, name="res%d_%d" % (n, half))
+                if half == 0:
+                    nc.scalar.copy(out=res[:], in_=tp[:, 0:2, :])
+                else:
+                    nc.vector.tensor_copy(out=res[:], in_=tp[:, 0:2, :])
+                nc.sync.dma_start(
+                    out=out[n, 2 * half * P : (2 * half + 2) * P, :].rearrange("(j p) o -> p j o", p=P),
+                    in_=res[:],
+                )
+
+        stage_a(0)
+        prepare(0)
+        stage_a(1)
+        prepare(1)
+        prepare(2)
+        multiply(0)
+        stage_b(0)
+        stage_b(1)
+        nc.vector.tensor_copy(out=bzf[:], in_=bz[:])
+        prepare(3)
+        multiply(1)
+        multiply(2)
+        prepare(4)
+        multiply(3)
+        prepare(5)
+        multiply(4)
+        prepare(6)
+
+        tail = list(range(first_lag[n_rounds - TAIL_ROUNDS], N_LAGS))
+        for l in tail:
+            mx_pass(l, 0)
+        evacuate(0)
+        for l in tail[:6]:
+            mx_pass(l, 1)
+        finish(0)
+        for l in tail[6:]:
+            mx_pass(l, 1)
+        evacuate(1)
+        finish(1)

@@ -26,7 +26,6 @@ XCOLS = N_BLK * Q
 
 ROUNDS = (2, 2, 4, 8, 12, 12, 11)
 N_BANKS = 6
-TAIL_ROUNDS = 2
 
 FLOPS = 2 * NB * T * N_LAGS * D * O
 
@@ -35,11 +34,6 @@ def tile_ctrf_kernel(tc, x, W, b, out):
     nc = tc.nc
     n_rounds = len(ROUNDS)
     first_lag = [sum(ROUNDS[:r]) for r in range(n_rounds)]
-    first_unit = [4 + sum([(n + 1) // 2 for n in ROUNDS[:r]]) for r in range(n_rounds)]
-    epi_unit = 4 + sum([(n + 1) // 2 for n in ROUNDS])
-    lag_round = []
-    for r in range(n_rounds):
-        lag_round.extend([r] * ROUNDS[r])
 
     with ExitStack() as ctx:
         keep = ctx.enter_context(tc.tile_pool(name="keep", bufs=1))
@@ -47,22 +41,28 @@ def tile_ctrf_kernel(tc, x, W, b, out):
         tpp = ctx.enter_context(tc.psum_pool(name="tpp", bufs=1))
         ctx.enter_context(tc.manual_schedule())
 
-        x_rows = x.rearrange("n t d -> (n t) d")
-        x_raw = []
-        for h in range(4):
-            xr = keep.tile([P, 2, D], BF16, name="x_raw%d" % h)
-            nc.sync.dma_start(
-                out=xr[:],
-                in_=x_rows[h * 256 : (h + 1) * 256, :].rearrange("(j p) d -> p j d", p=P),
-            )
-            x_raw.append(xr)
-        w_raw = []
-        for r in range(n_rounds):
+        x_raw = {}
+        w_raw = {}
+
+        def load_x(n):
+            for jt in range(4):
+                xr = keep.tile([P, D], BF16, name="x_raw%d_%d" % (n, jt))
+                nc.sync.dma_start(out=xr[:], in_=x[n, jt * P : (jt + 1) * P, :])
+                x_raw[(n, jt)] = xr
+
+        def load_w(r):
             wr = keep.tile([P, ROUNDS[r] * D], BF16, name="w_raw%d" % r)
             nc.sync.dma_start(
                 out=wr[:], in_=W[:, first_lag[r] * D : (first_lag[r] + ROUNDS[r]) * D]
             )
-            w_raw.append(wr)
+            w_raw[r] = wr
+
+        load_x(0)
+        load_w(0)
+        load_w(1)
+        load_x(1)
+        for r in range(2, n_rounds):
+            load_w(r)
 
         xe = []
         xq = []
@@ -91,24 +91,24 @@ def tile_ctrf_kernel(tc, x, W, b, out):
         for n in range(NB):
             acc.append(accp.tile([P, T], F32, name="acc%d" % n))
 
-        def bank(unit, shape):
+        units = {"next": 0}
+
+        def bank(shape):
+            unit = units["next"]
+            units["next"] = unit + 1
             return tpp.tile(shape, F32, name="tp_u%d" % unit, tag="tp%d" % (unit % N_BANKS))
 
-        for h in range(4):
-            n = h // 2
-            half = h % 2
-            tp = bank(h, [P, 2, 256])
-            xw = x_raw[h][:].bitcast(F32)
-            for j in range(2):
-                for u in range(2):
-                    nc.tensor.transpose(
-                        tp[:, u, j * P : (j + 1) * P], xw[:, j, u * P : (u + 1) * P], ident[:]
-                    )
+        def transpose_x(n):
             ew = xe[n][:].bitcast(F32).rearrange("p (r q u) -> p r q u", q=Q, u=2)
-            nc.scalar.copy(
-                out=ew[:, BASE : BASE + R, 8 * half : 8 * half + 8, :],
-                in_=tp[:].rearrange("p u (q r) -> p r q u", r=R),
-            )
+            for jt in range(4):
+                tp = bank([P, 2, P])
+                xw = x_raw[(n, jt)][:].bitcast(F32)
+                for u in range(2):
+                    nc.tensor.transpose(tp[:, u, :], xw[:, u * P : (u + 1) * P], ident[:])
+                nc.scalar.copy(
+                    out=ew[:, BASE : BASE + R, 4 * jt : 4 * jt + 4, :],
+                    in_=tp[:].rearrange("p u (q r) -> p r q u", r=R),
+                )
 
         def quantise_x(n, c0, width):
             nc.vector.quantize_mx(
@@ -125,17 +125,19 @@ def tile_ctrf_kernel(tc, x, W, b, out):
                     in_=xs[n][0][:, c0 + Q * j : end + Q * j].bitcast(I32),
                 )
 
-        def stage_a(n):
+        def upper_blocks(n):
             eb = xe[n][:].rearrange("p (r q e) -> p r q e", q=Q, e=4)
-            nc.vector.tensor_copy(
-                out=eb[:, BASE + R : N_BLK, 0 : Q - 1, :], in_=eb[:, BASE : BASE + N_BLK - BASE - R, 1:Q, :]
-            )
             quantise_x(n, BASE * Q, 512)
+            nc.vector.tensor_copy(
+                out=eb[:, BASE + R : N_BLK, 0 : Q - 1, :], in_=eb[:, BASE : N_BLK - R, 1:Q, :]
+            )
             quantise_x(n, BASE * Q + 512, 128)
             quantise_x(n, BASE * Q + 640, 32)
+
+        def upper_planes(n):
             shift_planes(n, BASE * Q, XCOLS)
 
-        def stage_b(n):
+        def lower_blocks(n):
             eb = xe[n][:].rearrange("p (r q e) -> p r q e", q=Q, e=4)
             nc.vector.tensor_copy(
                 out=eb[:, BASE - R : BASE, 1:Q, :], in_=eb[:, BASE : BASE + R, 0 : Q - 1, :]
@@ -145,6 +147,8 @@ def tile_ctrf_kernel(tc, x, W, b, out):
             )
             quantise_x(n, 0, 512)
             quantise_x(n, 512, 128)
+
+        def lower_planes(n):
             shift_planes(n, 0, BASE * Q)
 
         wq = {}
@@ -157,24 +161,19 @@ def tile_ctrf_kernel(tc, x, W, b, out):
             gw = g[:].bitcast(F32)
             for i0 in range(0, n, 2):
                 m = min(2, n - i0)
-                unit = first_unit[r] + i0 // 2
-                on_vector = n > 8 and (i0 // 2) % 3 == 2
-                tp = bank(unit, [P, 4, P])
+                tp = bank([P, 4, P])
                 for i in range(m):
                     for u in range(2):
                         col = (i0 + i) * WORDS + u * P
                         nc.tensor.transpose(tp[:, 2 * i + u, :], ww[:, col : col + P], ident[:])
                 if m == 1:
                     nc.tensor.transpose(tp[:, 2, :], bzf[:], ident[:])
-                dst = gw[:, i0 * WORDS : (i0 + m) * WORDS].rearrange("p (i o u) -> p i o u", i=m, u=2)
-                src = tp[:, 0 : 2 * m, :].rearrange("p (i u) o -> p i o u", u=2)
-                if on_vector:
-                    nc.vector.tensor_copy(out=dst, in_=src)
-                else:
-                    nc.scalar.copy(out=dst, in_=src)
+                nc.scalar.copy(
+                    out=gw[:, i0 * WORDS : (i0 + m) * WORDS].rearrange("p (i o u) -> p i o u", i=m, u=2),
+                    in_=tp[:, 0 : 2 * m, :].rearrange("p (i u) o -> p i o u", u=2),
+                )
                 if m == 1:
-                    assert on_vector
-                    nc.vector.tensor_copy(out=bias[:], in_=tp[:, 2, 0:1])
+                    nc.scalar.copy(out=bias[:], in_=tp[:, 2, 0:1])
             q = keep.tile([P, n * O], U32, name="wq%d" % r, align_bytes=64)
             s = keep.tile([P, n * O], U8, name="ws%d" % r, align_bytes=64)
             i0 = 0
@@ -189,26 +188,21 @@ def tile_ctrf_kernel(tc, x, W, b, out):
             wq[r] = q
             ws[r] = s
 
-        def mx_pass(l, n):
-            r = lag_round[l]
-            i = l - first_lag[r]
-            r0 = N_LAGS - 1 - l
-            j = r0 % 4
-            c0 = Q * (r0 - j)
-            nc.tensor.matmul_mx(
-                out=acc[n][:],
-                lhsT=wq[r][:, i * O : (i + 1) * O].bitcast(FP8X4),
-                lhsT_scale=ws[r][:, i * O : (i + 1) * O],
-                rhs=xq[n][:, Q * r0 : Q * r0 + T].bitcast(FP8X4),
-                rhs_scale=xs[n][j][:, c0 : c0 + T],
-                start=(l == 0),
-                stop=(l == N_LAGS - 1),
-            )
-
-        def multiply(r):
-            for n in range(NB):
-                for l in range(first_lag[r], first_lag[r] + ROUNDS[r]):
-                    mx_pass(l, n)
+        def multiply(n, r):
+            for i in range(ROUNDS[r]):
+                l = first_lag[r] + i
+                r0 = N_LAGS - 1 - l
+                j = r0 % 4
+                c0 = Q * (r0 - j)
+                nc.tensor.matmul_mx(
+                    out=acc[n][:],
+                    lhsT=wq[r][:, i * O : (i + 1) * O].bitcast(FP8X4),
+                    lhsT_scale=ws[r][:, i * O : (i + 1) * O],
+                    rhs=xq[n][:, Q * r0 : Q * r0 + T].bitcast(FP8X4),
+                    rhs_scale=xs[n][j][:, c0 : c0 + T],
+                    start=(l == 0),
+                    stop=(l == N_LAGS - 1),
+                )
 
         out_t = {}
 
@@ -223,47 +217,53 @@ def tile_ctrf_kernel(tc, x, W, b, out):
 
         def finish(n):
             for half in range(2):
-                unit = epi_unit + 2 * n + half
-                tp = bank(unit, [P, 4, P])
+                tp = bank([P, 2, P])
                 for j in range(2):
                     t0 = (2 * half + j) * P
                     nc.tensor.transpose(tp[:, j, :], out_t[n][:, t0 : t0 + P], ident[:])
                 res = keep.tile([P, 2, O], F32, name="res%d_%d" % (n, half))
-                if half == 0:
-                    nc.scalar.copy(out=res[:], in_=tp[:, 0:2, :])
+                if n == 1 and half == 1:
+                    nc.vector.tensor_copy(out=res[:], in_=tp[:])
                 else:
-                    nc.vector.tensor_copy(out=res[:], in_=tp[:, 0:2, :])
+                    nc.scalar.copy(out=res[:], in_=tp[:])
                 nc.sync.dma_start(
                     out=out[n, 2 * half * P : (2 * half + 2) * P, :].rearrange("(j p) o -> p j o", p=P),
                     in_=res[:],
                 )
 
-        stage_a(0)
+        transpose_x(0)
+        upper_blocks(0)
         prepare(0)
-        stage_a(1)
         prepare(1)
+        upper_planes(0)
+        transpose_x(1)
+        upper_blocks(1)
         prepare(2)
-        multiply(0)
-        stage_b(0)
-        stage_b(1)
-        nc.vector.tensor_copy(out=bzf[:], in_=bz[:])
+        upper_planes(1)
+        multiply(0, 0)
+        multiply(0, 1)
+        lower_blocks(0)
         prepare(3)
-        multiply(1)
-        multiply(2)
+        lower_planes(0)
+        multiply(1, 0)
+        multiply(1, 1)
+        multiply(1, 2)
+        lower_blocks(1)
         prepare(4)
-        multiply(3)
+        multiply(0, 2)
+        multiply(0, 3)
+        lower_planes(1)
+        nc.vector.tensor_copy(out=bzf[:], in_=bz[:])
         prepare(5)
-        multiply(4)
+        multiply(0, 4)
         prepare(6)
-
-        tail = list(range(first_lag[n_rounds - TAIL_ROUNDS], N_LAGS))
-        for l in tail:
-            mx_pass(l, 0)
+        multiply(1, 3)
+        multiply(1, 4)
+        multiply(0, 5)
+        multiply(0, 6)
         evacuate(0)
-        for l in tail[:6]:
-            mx_pass(l, 1)
-        finish(0)
-        for l in tail[6:]:
-            mx_pass(l, 1)
+        multiply(1, 5)
+        multiply(1, 6)
         evacuate(1)
+        finish(0)
         finish(1)

@@ -24,7 +24,7 @@ BASE = 40
 N_BLK = R + N_LAGS - 1
 XCOLS = N_BLK * Q
 
-ROUNDS = (2, 2, 4, 8, 12, 12, 11)
+ROUNDS = (2, 2, 4, 8, 8, 8, 8, 8, 3)
 N_BANKS = 6
 
 FLOPS = 2 * NB * T * N_LAGS * D * O
@@ -254,16 +254,14 @@ def tile_ctrf_kernel(tc, x, W, b, out):
         multiply(0, 3)
         lower_planes(1)
         nc.vector.tensor_copy(out=bzf[:], in_=bz[:])
-        prepare(5)
-        multiply(0, 4)
-        prepare(6)
-        multiply(1, 3)
-        multiply(1, 4)
-        multiply(0, 5)
-        multiply(0, 6)
+        for r in range(5, n_rounds):
+            prepare(r)
+            multiply(1, r - 2)
+            multiply(0, r - 1)
+        multiply(0, n_rounds - 1)
         evacuate(0)
-        multiply(1, 5)
-        multiply(1, 6)
+        multiply(1, n_rounds - 2)
+        multiply(1, n_rounds - 1)
         evacuate(1)
         finish(0)
         finish(1)

@@ -24,8 +24,9 @@ BASE = 40
 N_BLK = R + N_LAGS - 1
 XCOLS = N_BLK * Q
 
-ROUNDS = (2, 2, 4, 8, 8, 8, 8, 8, 3)
+ROUNDS = (2, 2, 4, 8, 12, 12, 11)
 N_BANKS = 6
+TAIL_ROUNDS = 2
 
 FLOPS = 2 * NB * T * N_LAGS * D * O
 
@@ -34,6 +35,11 @@ def tile_ctrf_kernel(tc, x, W, b, out):
     nc = tc.nc
     n_rounds = len(ROUNDS)
     first_lag = [sum(ROUNDS[:r]) for r in range(n_rounds)]
+    first_unit = [4 + sum([(n + 1) // 2 for n in ROUNDS[:r]]) for r in range(n_rounds)]
+    epi_unit = 4 + sum([(n + 1) // 2 for n in ROUNDS])
+    lag_round = []
+    for r in range(n_rounds):
+        lag_round.extend([r] * ROUNDS[r])
 
     with ExitStack() as ctx:
         keep = ctx.enter_context(tc.tile_pool(name="keep", bufs=1))
@@ -41,29 +47,25 @@ def tile_ctrf_kernel(tc, x, W, b, out):
         tpp = ctx.enter_context(tc.psum_pool(name="tpp", bufs=1))
         ctx.enter_context(tc.manual_schedule())
 
-        x_raw = {}
-        w_raw = {}
-
-        def load_x(n):
-            for jt in range(4):
-                xr = keep.tile([P, D], BF16, name="x_raw%d_%d" % (n, jt))
-                nc.sync.dma_start(out=xr[:], in_=x[n, jt * P : (jt + 1) * P, :])
-                x_raw[(n, jt)] = xr
-
-        def load_w(r):
+        x_rows = x.rearrange("n t d -> (n t) d")
+        x_raw = []
+        for h in range(4):
+            xr = keep.tile([P, 2, D], BF16, name="x_raw%d" % h)
+            nc.sync.dma_start(
+                out=xr[:],
+                in_=x_rows[h * 256 : (h + 1) * 256, :].rearrange("(j p) d -> p j d", p=P),
+            )
+            x_raw.append(xr)
+        w_raw = []
+        for r in range(n_rounds):
             wr = keep.tile([P, ROUNDS[r] * D], BF16, name="w_raw%d" % r)
             nc.sync.dma_start(
                 out=wr[:], in_=W[:, first_lag[r] * D : (first_lag[r] + ROUNDS[r]) * D]
             )
-            w_raw[r] = wr
+            w_raw.append(wr)
 
-        load_x(0)
-        load_w(0)
-        load_w(1)
-        load_x(1)
-        for r in range(2, n_rounds):
-            load_w(r)
-
+        dz = keep.tile([P, 512], BF16, name="dz")
+        nc.vector.memset(dz[:].bitcast(I32), 0)
         xe = []
         xq = []
         xs = []
@@ -91,24 +93,31 @@ def tile_ctrf_kernel(tc, x, W, b, out):
         for n in range(NB):
             acc.append(accp.tile([P, T], F32, name="acc%d" % n))
 
-        units = {"next": 0}
-
-        def bank(shape):
-            unit = units["next"]
-            units["next"] = unit + 1
+        def bank(unit, shape):
             return tpp.tile(shape, F32, name="tp_u%d" % unit, tag="tp%d" % (unit % N_BANKS))
 
-        def transpose_x(n):
-            ew = xe[n][:].bitcast(F32).rearrange("p (r q u) -> p r q u", q=Q, u=2)
-            for jt in range(4):
-                tp = bank([P, 2, P])
-                xw = x_raw[(n, jt)][:].bitcast(F32)
+        def keep_clock(count):
+            for k in range(count):
+                nc.tensor.matmul(out=acc[1][:], lhsT=dz[:, 0:P], rhs=dz[:], start=True, stop=True)
+
+        keep_clock(5)
+
+        for h in range(4):
+            n = h // 2
+            half = h % 2
+            tp = bank(h, [P, 2, 256])
+            xw = x_raw[h][:].bitcast(F32)
+            for j in range(2):
                 for u in range(2):
-                    nc.tensor.transpose(tp[:, u, :], xw[:, u * P : (u + 1) * P], ident[:])
-                nc.scalar.copy(
-                    out=ew[:, BASE : BASE + R, 4 * jt : 4 * jt + 4, :],
-                    in_=tp[:].rearrange("p u (q r) -> p r q u", r=R),
-                )
+                    nc.tensor.transpose(
+                        tp[:, u, j * P : (j + 1) * P], xw[:, j, u * P : (u + 1) * P], ident[:]
+                    )
+            ew = xe[n][:].bitcast(F32).rearrange("p (r q u) -> p r q u", q=Q, u=2)
+            nc.scalar.copy(
+                out=ew[:, BASE : BASE + R, 8 * half : 8 * half + 8, :],
+                in_=tp[:].rearrange("p u (q r) -> p r q u", r=R),
+            )
+            keep_clock(1)
 
         def quantise_x(n, c0, width):
             nc.vector.quantize_mx(
@@ -125,19 +134,17 @@ def tile_ctrf_kernel(tc, x, W, b, out):
                     in_=xs[n][0][:, c0 + Q * j : end + Q * j].bitcast(I32),
                 )
 
-        def upper_blocks(n):
+        def stage_a(n):
             eb = xe[n][:].rearrange("p (r q e) -> p r q e", q=Q, e=4)
-            quantise_x(n, BASE * Q, 512)
             nc.vector.tensor_copy(
-                out=eb[:, BASE + R : N_BLK, 0 : Q - 1, :], in_=eb[:, BASE : N_BLK - R, 1:Q, :]
+                out=eb[:, BASE + R : N_BLK, 0 : Q - 1, :], in_=eb[:, BASE : BASE + N_BLK - BASE - R, 1:Q, :]
             )
+            quantise_x(n, BASE * Q, 512)
             quantise_x(n, BASE * Q + 512, 128)
             quantise_x(n, BASE * Q + 640, 32)
-
-        def upper_planes(n):
             shift_planes(n, BASE * Q, XCOLS)
 
-        def lower_blocks(n):
+        def stage_b(n):
             eb = xe[n][:].rearrange("p (r q e) -> p r q e", q=Q, e=4)
             nc.vector.tensor_copy(
                 out=eb[:, BASE - R : BASE, 1:Q, :], in_=eb[:, BASE : BASE + R, 0 : Q - 1, :]
@@ -147,8 +154,6 @@ def tile_ctrf_kernel(tc, x, W, b, out):
             )
             quantise_x(n, 0, 512)
             quantise_x(n, 512, 128)
-
-        def lower_planes(n):
             shift_planes(n, 0, BASE * Q)
 
         wq = {}
@@ -161,19 +166,24 @@ def tile_ctrf_kernel(tc, x, W, b, out):
             gw = g[:].bitcast(F32)
             for i0 in range(0, n, 2):
                 m = min(2, n - i0)
-                tp = bank([P, 4, P])
+                unit = first_unit[r] + i0 // 2
+                on_vector = n > 8 and (i0 // 2) % 3 == 2
+                tp = bank(unit, [P, 4, P])
                 for i in range(m):
                     for u in range(2):
                         col = (i0 + i) * WORDS + u * P
                         nc.tensor.transpose(tp[:, 2 * i + u, :], ww[:, col : col + P], ident[:])
                 if m == 1:
                     nc.tensor.transpose(tp[:, 2, :], bzf[:], ident[:])
-                nc.scalar.copy(
-                    out=gw[:, i0 * WORDS : (i0 + m) * WORDS].rearrange("p (i o u) -> p i o u", i=m, u=2),
-                    in_=tp[:, 0 : 2 * m, :].rearrange("p (i u) o -> p i o u", u=2),
-                )
+                dst = gw[:, i0 * WORDS : (i0 + m) * WORDS].rearrange("p (i o u) -> p i o u", i=m, u=2)
+                src = tp[:, 0 : 2 * m, :].rearrange("p (i u) o -> p i o u", u=2)
+                if on_vector:
+                    nc.vector.tensor_copy(out=dst, in_=src)
+                else:
+                    nc.scalar.copy(out=dst, in_=src)
                 if m == 1:
-                    nc.scalar.copy(out=bias[:], in_=tp[:, 2, 0:1])
+                    assert on_vector
+                    nc.vector.tensor_copy(out=bias[:], in_=tp[:, 2, 0:1])
             q = keep.tile([P, n * O], U32, name="wq%d" % r, align_bytes=64)
             s = keep.tile([P, n * O], U8, name="ws%d" % r, align_bytes=64)
             i0 = 0
@@ -188,21 +198,26 @@ def tile_ctrf_kernel(tc, x, W, b, out):
             wq[r] = q
             ws[r] = s
 
-        def multiply(n, r):
-            for i in range(ROUNDS[r]):
-                l = first_lag[r] + i
-                r0 = N_LAGS - 1 - l
-                j = r0 % 4
-                c0 = Q * (r0 - j)
-                nc.tensor.matmul_mx(
-                    out=acc[n][:],
-                    lhsT=wq[r][:, i * O : (i + 1) * O].bitcast(FP8X4),
-                    lhsT_scale=ws[r][:, i * O : (i + 1) * O],
-                    rhs=xq[n][:, Q * r0 : Q * r0 + T].bitcast(FP8X4),
-                    rhs_scale=xs[n][j][:, c0 : c0 + T],
-                    start=(l == 0),
-                    stop=(l == N_LAGS - 1),
-                )
+        def mx_pass(l, n):
+            r = lag_round[l]
+            i = l - first_lag[r]
+            r0 = N_LAGS - 1 - l
+            j = r0 % 4
+            c0 = Q * (r0 - j)
+            nc.tensor.matmul_mx(
+                out=acc[n][:],
+                lhsT=wq[r][:, i * O : (i + 1) * O].bitcast(FP8X4),
+                lhsT_scale=ws[r][:, i * O : (i + 1) * O],
+                rhs=xq[n][:, Q * r0 : Q * r0 + T].bitcast(FP8X4),
+                rhs_scale=xs[n][j][:, c0 : c0 + T],
+                start=(l == 0),
+                stop=(l == N_LAGS - 1),
+            )
+
+        def multiply(r):
+            for n in range(NB):
+                for l in range(first_lag[r], first_lag[r] + ROUNDS[r]):
+                    mx_pass(l, n)
 
         out_t = {}
 
@@ -217,51 +232,50 @@ def tile_ctrf_kernel(tc, x, W, b, out):
 
         def finish(n):
             for half in range(2):
-                tp = bank([P, 2, P])
+                unit = epi_unit + 2 * n + half
+                tp = bank(unit, [P, 4, P])
                 for j in range(2):
                     t0 = (2 * half + j) * P
                     nc.tensor.transpose(tp[:, j, :], out_t[n][:, t0 : t0 + P], ident[:])
                 res = keep.tile([P, 2, O], F32, name="res%d_%d" % (n, half))
-                if n == 1 and half == 1:
-                    nc.vector.tensor_copy(out=res[:], in_=tp[:])
+                if half == 0:
+                    nc.scalar.copy(out=res[:], in_=tp[:, 0:2, :])
                 else:
-                    nc.scalar.copy(out=res[:], in_=tp[:])
+                    nc.vector.tensor_copy(out=res[:], in_=tp[:, 0:2, :])
                 nc.sync.dma_start(
                     out=out[n, 2 * half * P : (2 * half + 2) * P, :].rearrange("(j p) o -> p j o", p=P),
                     in_=res[:],
                 )
 
-        transpose_x(0)
-        upper_blocks(0)
+        stage_a(0)
         prepare(0)
+        keep_clock(1)
+        stage_a(1)
         prepare(1)
-        upper_planes(0)
-        transpose_x(1)
-        upper_blocks(1)
+        keep_clock(1)
         prepare(2)
-        upper_planes(1)
-        multiply(0, 0)
-        multiply(0, 1)
-        lower_blocks(0)
-        prepare(3)
-        lower_planes(0)
-        multiply(1, 0)
-        multiply(1, 1)
-        multiply(1, 2)
-        lower_blocks(1)
-        prepare(4)
-        multiply(0, 2)
-        multiply(0, 3)
-        lower_planes(1)
+        keep_clock(1)
+        multiply(0)
+        stage_b(0)
+        stage_b(1)
         nc.vector.tensor_copy(out=bzf[:], in_=bz[:])
-        for r in range(5, n_rounds):
-            prepare(r)
-            multiply(1, r - 2)
-            multiply(0, r - 1)
-        multiply(0, n_rounds - 1)
+        prepare(3)
+        multiply(1)
+        multiply(2)
+        prepare(4)
+        multiply(3)
+        prepare(5)
+        multiply(4)
+        prepare(6)
+
+        tail = list(range(first_lag[n_rounds - TAIL_ROUNDS], N_LAGS))
+        for l in tail:
+            mx_pass(l, 0)
         evacuate(0)
-        multiply(1, n_rounds - 2)
-        multiply(1, n_rounds - 1)
-        evacuate(1)
+        for l in tail[:6]:
+            mx_pass(l, 1)
         finish(0)
+        for l in tail[6:]:
+            mx_pass(l, 1)
+        evacuate(1)
         finish(1)

@@ -45,7 +45,6 @@ def tile_ctrf_kernel(tc, x, W, b, out):
         keep = ctx.enter_context(tc.tile_pool(name="keep", bufs=1))
         accp = ctx.enter_context(tc.psum_pool(name="accp", bufs=1))
         tpp = ctx.enter_context(tc.psum_pool(name="tpp", bufs=1))
-        ctx.enter_context(tc.manual_schedule())
 
         x_rows = x.rearrange("n t d -> (n t) d")
         x_raw = []
@@ -64,8 +63,6 @@ def tile_ctrf_kernel(tc, x, W, b, out):
             )
             w_raw.append(wr)
 
-        dz = keep.tile([P, 512], BF16, name="dz")
-        nc.vector.memset(dz[:].bitcast(I32), 0)
         xe = []
         xq = []
         xs = []
@@ -96,12 +93,6 @@ def tile_ctrf_kernel(tc, x, W, b, out):
         def bank(unit, shape):
             return tpp.tile(shape, F32, name="tp_u%d" % unit, tag="tp%d" % (unit % N_BANKS))
 
-        def keep_clock(count):
-            for k in range(count):
-                nc.tensor.matmul(out=acc[1][:], lhsT=dz[:, 0:P], rhs=dz[:], start=True, stop=True)
-
-        keep_clock(5)
-
         for h in range(4):
             n = h // 2
             half = h % 2
@@ -117,7 +108,6 @@ def tile_ctrf_kernel(tc, x, W, b, out):
                 out=ew[:, BASE : BASE + R, 8 * half : 8 * half + 8, :],
                 in_=tp[:].rearrange("p u (q r) -> p r q u", r=R),
             )
-            keep_clock(1)
 
         def quantise_x(n, c0, width):
             nc.vector.quantize_mx(
@@ -249,12 +239,9 @@ def tile_ctrf_kernel(tc, x, W, b, out):
 
         stage_a(0)
         prepare(0)
-        keep_clock(1)
         stage_a(1)
         prepare(1)
-        keep_clock(1)
         prepare(2)
-        keep_clock(1)
         multiply(0)
         stage_b(0)
         stage_b(1)

@@ -11,32 +11,41 @@ I32 = mybir.dt.int32
 FP8X4 = mybir.dt.float8_e4m3fn_x4
 
 P = 128
+PACK = 4
 N_LAGS = 51
 D = 512
 T = 512
-NB = 2
+BATCHES = 2
 O = 128
 WORDS = D // 2
 
-Q = 16
-R = 32
+STRIP = 16
+WINDOW = T // STRIP
 BASE = 40
-N_BLK = R + N_LAGS - 1
-XCOLS = N_BLK * Q
+N_STRIPS = WINDOW + N_LAGS - 1
+XCOLS = N_STRIPS * STRIP
+N_PLANES = 64 // STRIP
+
+X_PART = 256
+X_PARTS = BATCHES * T // X_PART
 
 ROUNDS = (2, 2, 4, 8, 12, 12, 11)
+BANK_LAGS = 2
 N_BANKS = 6
 TAIL_ROUNDS = 2
+HOLD = 6
+CLOCK_START = 5
 
-FLOPS = 2 * NB * T * N_LAGS * D * O
+FLOPS = 2 * BATCHES * T * N_LAGS * D * O
 
 
 def tile_ctrf_kernel(tc, x, W, b, out):
     nc = tc.nc
     n_rounds = len(ROUNDS)
     first_lag = [sum(ROUNDS[:r]) for r in range(n_rounds)]
-    first_unit = [4 + sum([(n + 1) // 2 for n in ROUNDS[:r]]) for r in range(n_rounds)]
-    epi_unit = 4 + sum([(n + 1) // 2 for n in ROUNDS])
+    round_units = [(lags + BANK_LAGS - 1) // BANK_LAGS for lags in ROUNDS]
+    first_unit = [X_PARTS + sum(round_units[:r]) for r in range(n_rounds)]
+    out_unit = X_PARTS + sum(round_units)
     lag_round = []
     for r in range(n_rounds):
         lag_round.extend([r] * ROUNDS[r])
@@ -45,14 +54,15 @@ def tile_ctrf_kernel(tc, x, W, b, out):
         keep = ctx.enter_context(tc.tile_pool(name="keep", bufs=1))
         accp = ctx.enter_context(tc.psum_pool(name="accp", bufs=1))
         tpp = ctx.enter_context(tc.psum_pool(name="tpp", bufs=1))
+        ctx.enter_context(tc.manual_schedule())
 
         x_rows = x.rearrange("n t d -> (n t) d")
         x_raw = []
-        for h in range(4):
-            xr = keep.tile([P, 2, D], BF16, name="x_raw%d" % h)
+        for part in range(X_PARTS):
+            xr = keep.tile([P, X_PART // P, D], BF16, name="x_raw%d" % part)
             nc.sync.dma_start(
                 out=xr[:],
-                in_=x_rows[h * 256 : (h + 1) * 256, :].rearrange("(j p) d -> p j d", p=P),
+                in_=x_rows[part * X_PART : (part + 1) * X_PART, :].rearrange("(j p) d -> p j d", p=P),
             )
             x_raw.append(xr)
         w_raw = []
@@ -63,149 +73,173 @@ def tile_ctrf_kernel(tc, x, W, b, out):
             )
             w_raw.append(wr)
 
-        xe = []
-        xq = []
-        xs = []
-        for n in range(NB):
-            e = keep.tile([P, XCOLS * 4], BF16, name="xe%d" % n, align_bytes=64)
-            ei = e[:].bitcast(I32).rearrange("p (r q u) -> p r q u", q=Q, u=2)
-            nc.vector.memset(ei[:, 0:BASE, 0:2, :], 0)
-            nc.vector.memset(ei[:, BASE + R : N_BLK, Q - 1 : Q, :], 0)
-            xe.append(e)
-            xq.append(keep.tile([P, XCOLS], U32, name="xq%d" % n, align_bytes=64))
+        zeros = keep.tile([P, T], BF16, name="dz")
+        nc.vector.memset(zeros[:].bitcast(I32), 0)
+        x_strips = []
+        x_codes = []
+        x_planes = []
+        for n in range(BATCHES):
+            strips = keep.tile([P, XCOLS * PACK], BF16, name="xe%d" % n, align_bytes=64)
+            as_int = strips[:].bitcast(I32).rearrange("p (s c u) -> p s c u", c=STRIP, u=2)
+            nc.vector.memset(as_int[:, 0:BASE, 0:2, :], 0)
+            nc.vector.memset(as_int[:, BASE + WINDOW : N_STRIPS, STRIP - 1 : STRIP, :], 0)
+            x_strips.append(strips)
+            x_codes.append(keep.tile([P, XCOLS], U32, name="xq%d" % n, align_bytes=64))
             planes = []
-            for j in range(4):
-                planes.append(keep.tile([P, XCOLS], U8, name="xs%d_%d" % (n, j), align_bytes=64))
+            for shift in range(N_PLANES):
+                planes.append(keep.tile([P, XCOLS], U8, name="xs%d_%d" % (n, shift), align_bytes=64))
             nc.vector.memset(planes[0][:].bitcast(I32), 0)
-            xs.append(planes)
+            x_planes.append(planes)
         ident = keep.tile([P, P], F32, name="ident")
         make_identity(nc, ident[:])
-        bz = keep.tile([P, P], BF16, name="bz")
-        nc.vector.memset(bz[:], 0.0)
-        nc.scalar.dma_start(out=bz[0:1, :], in_=b.rearrange("(a o) -> a o", a=1))
-        bzf = keep.tile([P, P], F32, name="bzf")
+        bias_row = keep.tile([P, P], BF16, name="bz")
+        nc.vector.memset(bias_row[:], 0.0)
+        nc.scalar.dma_start(out=bias_row[0:1, :], in_=b.rearrange("(a o) -> a o", a=1))
+        bias_row_f32 = keep.tile([P, P], F32, name="bzf")
         bias = keep.tile([P, 1], F32, name="bias")
 
         acc = []
-        for n in range(NB):
+        for n in range(BATCHES):
             acc.append(accp.tile([P, T], F32, name="acc%d" % n))
 
         def bank(unit, shape):
             return tpp.tile(shape, F32, name="tp_u%d" % unit, tag="tp%d" % (unit % N_BANKS))
 
-        for h in range(4):
-            n = h // 2
-            half = h % 2
-            tp = bank(h, [P, 2, 256])
-            xw = x_raw[h][:].bitcast(F32)
-            for j in range(2):
+        def keep_clock(count):
+            for rep in range(count):
+                nc.tensor.matmul(out=acc[1][:], lhsT=zeros[:, 0:P], rhs=zeros[:], start=True, stop=True)
+
+        keep_clock(CLOCK_START)
+
+        part_cols = X_PART // WINDOW
+        for part in range(X_PARTS):
+            n = part * X_PART // T
+            c0 = (part * X_PART % T) // WINDOW
+            tp = bank(part, [P, 2, X_PART])
+            x_words = x_raw[part][:].bitcast(F32)
+            for j in range(X_PART // P):
                 for u in range(2):
                     nc.tensor.transpose(
-                        tp[:, u, j * P : (j + 1) * P], xw[:, j, u * P : (u + 1) * P], ident[:]
+                        tp[:, u, j * P : (j + 1) * P], x_words[:, j, u * P : (u + 1) * P], ident[:]
                     )
-            ew = xe[n][:].bitcast(F32).rearrange("p (r q u) -> p r q u", q=Q, u=2)
+            as_words = x_strips[n][:].bitcast(F32).rearrange("p (s c u) -> p s c u", c=STRIP, u=2)
             nc.scalar.copy(
-                out=ew[:, BASE : BASE + R, 8 * half : 8 * half + 8, :],
-                in_=tp[:].rearrange("p u (q r) -> p r q u", r=R),
+                out=as_words[:, BASE : BASE + WINDOW, c0 : c0 + part_cols, :],
+                in_=tp[:].rearrange("p u (c s) -> p s c u", s=WINDOW),
             )
+            if c0 + part_cols == STRIP:
+                nc.scalar.copy(
+                    out=as_words[:, BASE + WINDOW : N_STRIPS, 0 : STRIP - 1, :],
+                    in_=as_words[:, BASE : N_STRIPS - WINDOW, 1:STRIP, :],
+                )
+            keep_clock(1)
 
-        def quantise_x(n, c0, width):
+        def quantise_x(n, col, width):
             nc.vector.quantize_mx(
-                out=xq[n][:, c0 : c0 + width].bitcast(FP8X4),
-                scales=xs[n][0][:, c0 : c0 + width],
-                in_=xe[n][:, 4 * c0 : 4 * (c0 + width)],
+                out=x_codes[n][:, col : col + width].bitcast(FP8X4),
+                scales=x_planes[n][0][:, col : col + width],
+                in_=x_strips[n][:, PACK * col : PACK * (col + width)],
             )
 
-        def shift_planes(n, c0, c1):
-            for j in range(1, 4):
-                end = min(c1, XCOLS - Q * j)
+        def shift_planes(n, col, col_end):
+            for shift in range(1, N_PLANES):
+                end = min(col_end, XCOLS - STRIP * shift)
                 nc.vector.tensor_copy(
-                    out=xs[n][j][:, c0:end].bitcast(I32),
-                    in_=xs[n][0][:, c0 + Q * j : end + Q * j].bitcast(I32),
+                    out=x_planes[n][shift][:, col:end].bitcast(I32),
+                    in_=x_planes[n][0][:, col + STRIP * shift : end + STRIP * shift].bitcast(I32),
                 )
 
-        def stage_a(n):
-            eb = xe[n][:].rearrange("p (r q e) -> p r q e", q=Q, e=4)
-            nc.vector.tensor_copy(
-                out=eb[:, BASE + R : N_BLK, 0 : Q - 1, :], in_=eb[:, BASE : BASE + N_BLK - BASE - R, 1:Q, :]
-            )
-            quantise_x(n, BASE * Q, 512)
-            quantise_x(n, BASE * Q + 512, 128)
-            quantise_x(n, BASE * Q + 640, 32)
-            shift_planes(n, BASE * Q, XCOLS)
+        def upper_strips(n):
+            quantise_x(n, BASE * STRIP, 512)
+            quantise_x(n, BASE * STRIP + 512, 128)
+            quantise_x(n, BASE * STRIP + 640, 32)
 
-        def stage_b(n):
-            eb = xe[n][:].rearrange("p (r q e) -> p r q e", q=Q, e=4)
+        def upper_planes(n):
+            shift_planes(n, BASE * STRIP, XCOLS)
+
+        def lower_strips(n):
+            view = x_strips[n][:].rearrange("p (s c e) -> p s c e", c=STRIP, e=PACK)
             nc.vector.tensor_copy(
-                out=eb[:, BASE - R : BASE, 1:Q, :], in_=eb[:, BASE : BASE + R, 0 : Q - 1, :]
+                out=view[:, BASE - WINDOW : BASE, 1:STRIP, :], in_=view[:, BASE : BASE + WINDOW, 0 : STRIP - 1, :]
             )
             nc.vector.tensor_copy(
-                out=eb[:, 0 : BASE - R, 2:Q, :], in_=eb[:, 2 * R : BASE + R, 0 : Q - 2, :]
+                out=view[:, 0 : BASE - WINDOW, 2:STRIP, :], in_=view[:, 2 * WINDOW : BASE + WINDOW, 0 : STRIP - 2, :]
             )
             quantise_x(n, 0, 512)
             quantise_x(n, 512, 128)
-            shift_planes(n, 0, BASE * Q)
+            shift_planes(n, 0, BASE * STRIP)
 
-        wq = {}
-        ws = {}
+        w_codes = {}
+        w_planes = {}
+
+        w_grouped = {}
 
         def prepare(r):
-            n = ROUNDS[r]
-            ww = w_raw[r][:].bitcast(F32)
-            g = keep.tile([P, n * D], BF16, name="wg%d" % r, align_bytes=64)
-            gw = g[:].bitcast(F32)
-            for i0 in range(0, n, 2):
-                m = min(2, n - i0)
-                unit = first_unit[r] + i0 // 2
-                on_vector = n > 8 and (i0 // 2) % 3 == 2
-                tp = bank(unit, [P, 4, P])
+            transpose_w(r)
+            quantise_w(r)
+
+        def transpose_w(r):
+            lags = ROUNDS[r]
+            w_words = w_raw[r][:].bitcast(F32)
+            grouped = keep.tile([P, lags * D], BF16, name="wg%d" % r, align_bytes=64)
+            w_grouped[r] = grouped
+            grouped_words = grouped[:].bitcast(F32)
+            for i0 in range(0, lags, BANK_LAGS):
+                m = min(BANK_LAGS, lags - i0)
+                unit = first_unit[r] + i0 // BANK_LAGS
+                on_vector = round_units[r] == N_BANKS and (i0 // BANK_LAGS) % 3 == 2
+                tp = bank(unit, [P, 2 * BANK_LAGS, P])
                 for i in range(m):
                     for u in range(2):
-                        col = (i0 + i) * WORDS + u * P
-                        nc.tensor.transpose(tp[:, 2 * i + u, :], ww[:, col : col + P], ident[:])
-                if m == 1:
-                    nc.tensor.transpose(tp[:, 2, :], bzf[:], ident[:])
-                dst = gw[:, i0 * WORDS : (i0 + m) * WORDS].rearrange("p (i o u) -> p i o u", i=m, u=2)
+                        word = (i0 + i) * WORDS + u * P
+                        nc.tensor.transpose(tp[:, 2 * i + u, :], w_words[:, word : word + P], ident[:])
+                if m < BANK_LAGS:
+                    nc.tensor.transpose(tp[:, 2 * m, :], bias_row_f32[:], ident[:])
+                dst = grouped_words[:, i0 * WORDS : (i0 + m) * WORDS].rearrange("p (i o u) -> p i o u", i=m, u=2)
                 src = tp[:, 0 : 2 * m, :].rearrange("p (i u) o -> p i o u", u=2)
                 if on_vector:
                     nc.vector.tensor_copy(out=dst, in_=src)
                 else:
                     nc.scalar.copy(out=dst, in_=src)
-                if m == 1:
+                if m < BANK_LAGS:
                     assert on_vector
-                    nc.vector.tensor_copy(out=bias[:], in_=tp[:, 2, 0:1])
-            q = keep.tile([P, n * O], U32, name="wq%d" % r, align_bytes=64)
-            s = keep.tile([P, n * O], U8, name="ws%d" % r, align_bytes=64)
+                    nc.vector.tensor_copy(out=bias[:], in_=tp[:, 2 * m, 0:1])
+
+        def quantise_w(r):
+            lags = ROUNDS[r]
+            grouped = w_grouped[r]
+            codes = keep.tile([P, lags * O], U32, name="wq%d" % r, align_bytes=64)
+            plane = keep.tile([P, lags * O], U8, name="ws%d" % r, align_bytes=64)
             i0 = 0
             for m in (8, 4, 2, 1):
-                if n - i0 >= m:
+                if lags - i0 >= m:
                     nc.vector.quantize_mx(
-                        out=q[:, i0 * O : (i0 + m) * O].bitcast(FP8X4),
-                        scales=s[:, i0 * O : (i0 + m) * O],
-                        in_=g[:, i0 * D : (i0 + m) * D],
+                        out=codes[:, i0 * O : (i0 + m) * O].bitcast(FP8X4),
+                        scales=plane[:, i0 * O : (i0 + m) * O],
+                        in_=grouped[:, i0 * D : (i0 + m) * D],
                     )
                     i0 += m
-            wq[r] = q
-            ws[r] = s
+            w_codes[r] = codes
+            w_planes[r] = plane
 
         def mx_pass(l, n):
             r = lag_round[l]
             i = l - first_lag[r]
-            r0 = N_LAGS - 1 - l
-            j = r0 % 4
-            c0 = Q * (r0 - j)
+            s0 = N_LAGS - 1 - l
+            shift = s0 % N_PLANES
+            plane_col = STRIP * (s0 - shift)
             nc.tensor.matmul_mx(
                 out=acc[n][:],
-                lhsT=wq[r][:, i * O : (i + 1) * O].bitcast(FP8X4),
-                lhsT_scale=ws[r][:, i * O : (i + 1) * O],
-                rhs=xq[n][:, Q * r0 : Q * r0 + T].bitcast(FP8X4),
-                rhs_scale=xs[n][j][:, c0 : c0 + T],
+                lhsT=w_codes[r][:, i * O : (i + 1) * O].bitcast(FP8X4),
+                lhsT_scale=w_planes[r][:, i * O : (i + 1) * O],
+                rhs=x_codes[n][:, STRIP * s0 : STRIP * s0 + T].bitcast(FP8X4),
+                rhs_scale=x_planes[n][shift][:, plane_col : plane_col + T],
                 start=(l == 0),
                 stop=(l == N_LAGS - 1),
             )
 
         def multiply(r):
-            for n in range(NB):
+            for n in range(BATCHES):
                 for l in range(first_lag[r], first_lag[r] + ROUNDS[r]):
                     mx_pass(l, n)
 
@@ -214,38 +248,44 @@ def tile_ctrf_kernel(tc, x, W, b, out):
         def evacuate(n):
             o_t = keep.tile([P, T], F32, name="out_t%d" % n)
             nc.vector.tensor_scalar_add(
-                out=o_t[:].rearrange("p (q r) -> p q r", r=R),
-                in0=acc[n][:].rearrange("p (r q) -> p q r", q=Q),
+                out=o_t[:].rearrange("p (c w) -> p c w", w=WINDOW),
+                in0=acc[n][:].rearrange("p (w c) -> p c w", c=STRIP),
                 scalar1=bias[:, 0:1],
             )
             out_t[n] = o_t
 
         def finish(n):
-            for half in range(2):
-                unit = epi_unit + 2 * n + half
-                tp = bank(unit, [P, 4, P])
+            for pair in range(2):
+                unit = out_unit + 2 * n + pair
+                tp = bank(unit, [P, 2 * BANK_LAGS, P])
                 for j in range(2):
-                    t0 = (2 * half + j) * P
+                    t0 = (2 * pair + j) * P
                     nc.tensor.transpose(tp[:, j, :], out_t[n][:, t0 : t0 + P], ident[:])
-                res = keep.tile([P, 2, O], F32, name="res%d_%d" % (n, half))
-                if half == 0:
+                res = keep.tile([P, 2, O], F32, name="res%d_%d" % (n, pair))
+                if pair == 0:
                     nc.scalar.copy(out=res[:], in_=tp[:, 0:2, :])
                 else:
                     nc.vector.tensor_copy(out=res[:], in_=tp[:, 0:2, :])
                 nc.sync.dma_start(
-                    out=out[n, 2 * half * P : (2 * half + 2) * P, :].rearrange("(j p) o -> p j o", p=P),
+                    out=out[n, 2 * pair * P : (2 * pair + 2) * P, :].rearrange("(j p) o -> p j o", p=P),
                     in_=res[:],
                 )
 
-        stage_a(0)
-        prepare(0)
-        stage_a(1)
+        upper_strips(0)
+        upper_planes(0)
+        transpose_w(0)
+        keep_clock(1)
+        upper_strips(1)
+        quantise_w(0)
+        upper_planes(1)
         prepare(1)
+        keep_clock(1)
         prepare(2)
+        keep_clock(1)
         multiply(0)
-        stage_b(0)
-        stage_b(1)
-        nc.vector.tensor_copy(out=bzf[:], in_=bz[:])
+        lower_strips(0)
+        lower_strips(1)
+        nc.vector.tensor_copy(out=bias_row_f32[:], in_=bias_row[:])
         prepare(3)
         multiply(1)
         multiply(2)
@@ -259,10 +299,10 @@ def tile_ctrf_kernel(tc, x, W, b, out):
         for l in tail:
             mx_pass(l, 0)
         evacuate(0)
-        for l in tail[:6]:
+        for l in tail[:HOLD]:
             mx_pass(l, 1)
         finish(0)
-        for l in tail[6:]:
+        for l in tail[HOLD:]:
             mx_pass(l, 1)
         evacuate(1)
         finish(1)

from contextlib import ExitStack

import concourse.mybir as mybir
from concourse.masks import make_identity

F32 = mybir.dt.float32
BF16 = mybir.dt.bfloat16
U32 = mybir.dt.uint32
U8 = mybir.dt.uint8
I32 = mybir.dt.int32
FP8X4 = mybir.dt.float8_e4m3fn_x4

P = 128
PACK = 4
N_LAGS = 51
D = 512
T = 512
BATCHES = 2
O = 128
WORDS = D // 2

STRIP = 16
WINDOW = T // STRIP
BASE = 40
N_STRIPS = WINDOW + N_LAGS - 1
XCOLS = N_STRIPS * STRIP
N_PLANES = 64 // STRIP

X_PART = 256
X_PARTS = BATCHES * T // X_PART

ROUNDS = (2, 2, 4, 8, 12, 12, 11)
BANK_LAGS = 2
N_BANKS = 6
TAIL_ROUNDS = 2
HOLD = 6
CLOCK_START = 5

FLOPS = 2 * BATCHES * T * N_LAGS * D * O


def tile_ctrf_kernel(tc, x, W, b, out):
    nc = tc.nc
    n_rounds = len(ROUNDS)
    first_lag = [sum(ROUNDS[:r]) for r in range(n_rounds)]
    round_units = [(lags + BANK_LAGS - 1) // BANK_LAGS for lags in ROUNDS]
    first_unit = [X_PARTS + sum(round_units[:r]) for r in range(n_rounds)]
    out_unit = X_PARTS + sum(round_units)
    lag_round = []
    for r in range(n_rounds):
        lag_round.extend([r] * ROUNDS[r])

    with ExitStack() as ctx:
        keep = ctx.enter_context(tc.tile_pool(name="keep", bufs=1))
        accp = ctx.enter_context(tc.psum_pool(name="accp", bufs=1))
        tpp = ctx.enter_context(tc.psum_pool(name="tpp", bufs=1))
        ctx.enter_context(tc.manual_schedule())

        x_rows = x.rearrange("n t d -> (n t) d")
        x_raw = []
        for part in range(X_PARTS):
            xr = keep.tile([P, X_PART // P, D], BF16, name="x_raw%d" % part)
            nc.sync.dma_start(
                out=xr[:],
                in_=x_rows[part * X_PART : (part + 1) * X_PART, :].rearrange("(j p) d -> p j d", p=P),
            )
            x_raw.append(xr)
        w_raw = []
        for r in range(n_rounds):
            wr = keep.tile([P, ROUNDS[r] * D], BF16, name="w_raw%d" % r)
            nc.sync.dma_start(
                out=wr[:], in_=W[:, first_lag[r] * D : (first_lag[r] + ROUNDS[r]) * D]
            )
            w_raw.append(wr)

        zeros = keep.tile([P, T], BF16, name="dz")
        nc.vector.memset(zeros[:].bitcast(I32), 0)
        x_strips = []
        x_codes = []
        x_planes = []
        for n in range(BATCHES):
            strips = keep.tile([P, XCOLS * PACK], BF16, name="xe%d" % n, align_bytes=64)
            as_int = strips[:].bitcast(I32).rearrange("p (s c u) -> p s c u", c=STRIP, u=2)
            nc.vector.memset(as_int[:, 0:BASE, 0:2, :], 0)
            nc.vector.memset(as_int[:, BASE + WINDOW : N_STRIPS, STRIP - 1 : STRIP, :], 0)
            x_strips.append(strips)
            x_codes.append(keep.tile([P, XCOLS], U32, name="xq%d" % n, align_bytes=64))
            planes = []
            for shift in range(N_PLANES):
                planes.append(keep.tile([P, XCOLS], U8, name="xs%d_%d" % (n, shift), align_bytes=64))
            nc.vector.memset(planes[0][:].bitcast(I32), 0)
            x_planes.append(planes)
        ident = keep.tile([P, P], F32, name="ident")
        make_identity(nc, ident[:])
        bias_row = keep.tile([P, P], BF16, name="bz")
        nc.vector.memset(bias_row[:], 0.0)
        nc.scalar.dma_start(out=bias_row[0:1, :], in_=b.rearrange("(a o) -> a o", a=1))
        bias_row_f32 = keep.tile([P, P], F32, name="bzf")
        bias = keep.tile([P, 1], F32, name="bias")

        acc = []
        for n in range(BATCHES):
            acc.append(accp.tile([P, T], F32, name="acc%d" % n))

        def bank(unit, shape):
            return tpp.tile(shape, F32, name="tp_u%d" % unit, tag="tp%d" % (unit % N_BANKS))

        def keep_clock(count):
            for rep in range(count):
                nc.tensor.matmul(out=acc[1][:], lhsT=zeros[:, 0:P], rhs=zeros[:], start=True, stop=True)

        keep_clock(CLOCK_START)

        part_cols = X_PART // WINDOW
        for part in range(X_PARTS):
            n = part * X_PART // T
            c0 = (part * X_PART % T) // WINDOW
            tp = bank(part, [P, 2, X_PART])
            x_words = x_raw[part][:].bitcast(F32)
            for j in range(X_PART // P):
                for u in range(2):
                    nc.tensor.transpose(
                        tp[:, u, j * P : (j + 1) * P], x_words[:, j, u * P : (u + 1) * P], ident[:]
                    )
            as_words = x_strips[n][:].bitcast(F32).rearrange("p (s c u) -> p s c u", c=STRIP, u=2)
            nc.scalar.copy(
                out=as_words[:, BASE : BASE + WINDOW, c0 : c0 + part_cols, :],
                in_=tp[:].rearrange("p u (c s) -> p s c u", s=WINDOW),
            )
            if c0 + part_cols == STRIP:
                nc.scalar.copy(
                    out=as_words[:, BASE + WINDOW : N_STRIPS, 0 : STRIP - 1, :],
                    in_=as_words[:, BASE : N_STRIPS - WINDOW, 1:STRIP, :],
                )
            keep_clock(1)

        def quantise_x(n, col, width):
            nc.vector.quantize_mx(
                out=x_codes[n][:, col : col + width].bitcast(FP8X4),
                scales=x_planes[n][0][:, col : col + width],
                in_=x_strips[n][:, PACK * col : PACK * (col + width)],
            )

        def shift_planes(n, col, col_end):
            for shift in range(1, N_PLANES):
                end = min(col_end, XCOLS - STRIP * shift)
                nc.vector.tensor_copy(
                    out=x_planes[n][shift][:, col:end].bitcast(I32),
                    in_=x_planes[n][0][:, col + STRIP * shift : end + STRIP * shift].bitcast(I32),
                )

        def upper_strips(n):
            quantise_x(n, BASE * STRIP, 512)
            quantise_x(n, BASE * STRIP + 512, 128)
            quantise_x(n, BASE * STRIP + 640, 32)

        def upper_planes(n):
            shift_planes(n, BASE * STRIP, XCOLS)

        def lower_strips(n):
            view = x_strips[n][:].rearrange("p (s c e) -> p s c e", c=STRIP, e=PACK)
            nc.vector.tensor_copy(
                out=view[:, BASE - WINDOW : BASE, 1:STRIP, :], in_=view[:, BASE : BASE + WINDOW, 0 : STRIP - 1, :]
            )
            nc.vector.tensor_copy(
                out=view[:, 0 : BASE - WINDOW, 2:STRIP, :], in_=view[:, 2 * WINDOW : BASE + WINDOW, 0 : STRIP - 2, :]
            )
            quantise_x(n, 0, 512)
            quantise_x(n, 512, 128)
            shift_planes(n, 0, BASE * STRIP)

        w_codes = {}
        w_planes = {}

        w_grouped = {}

        def prepare(r):
            transpose_w(r)
            quantise_w(r)

        def transpose_w(r):
            lags = ROUNDS[r]
            w_words = w_raw[r][:].bitcast(F32)
            grouped = keep.tile([P, lags * D], BF16, name="wg%d" % r, align_bytes=64)
            w_grouped[r] = grouped
            grouped_words = grouped[:].bitcast(F32)
            for i0 in range(0, lags, BANK_LAGS):
                m = min(BANK_LAGS, lags - i0)
                unit = first_unit[r] + i0 // BANK_LAGS
                on_vector = round_units[r] == N_BANKS and (i0 // BANK_LAGS) % 3 == 2
                tp = bank(unit, [P, 2 * BANK_LAGS, P])
                for i in range(m):
                    for u in range(2):
                        word = (i0 + i) * WORDS + u * P
                        nc.tensor.transpose(tp[:, 2 * i + u, :], w_words[:, word : word + P], ident[:])
                if m < BANK_LAGS:
                    nc.tensor.transpose(tp[:, 2 * m, :], bias_row_f32[:], ident[:])
                dst = grouped_words[:, i0 * WORDS : (i0 + m) * WORDS].rearrange("p (i o u) -> p i o u", i=m, u=2)
                src = tp[:, 0 : 2 * m, :].rearrange("p (i u) o -> p i o u", u=2)
                if on_vector:
                    nc.vector.tensor_copy(out=dst, in_=src)
                else:
                    nc.scalar.copy(out=dst, in_=src)
                if m < BANK_LAGS:
                    assert on_vector
                    nc.vector.tensor_copy(out=bias[:], in_=tp[:, 2 * m, 0:1])

        def quantise_w(r):
            lags = ROUNDS[r]
            grouped = w_grouped[r]
            codes = keep.tile([P, lags * O], U32, name="wq%d" % r, align_bytes=64)
            plane = keep.tile([P, lags * O], U8, name="ws%d" % r, align_bytes=64)
            i0 = 0
            for m in (8, 4, 2, 1):
                if lags - i0 >= m:
                    nc.vector.quantize_mx(
                        out=codes[:, i0 * O : (i0 + m) * O].bitcast(FP8X4),
                        scales=plane[:, i0 * O : (i0 + m) * O],
                        in_=grouped[:, i0 * D : (i0 + m) * D],
                    )
                    i0 += m
            w_codes[r] = codes
            w_planes[r] = plane

        def mx_pass(l, n):
            r = lag_round[l]
            i = l - first_lag[r]
            s0 = N_LAGS - 1 - l
            shift = s0 % N_PLANES
            plane_col = STRIP * (s0 - shift)
            nc.tensor.matmul_mx(
                out=acc[n][:],
                lhsT=w_codes[r][:, i * O : (i + 1) * O].bitcast(FP8X4),
                lhsT_scale=w_planes[r][:, i * O : (i + 1) * O],
                rhs=x_codes[n][:, STRIP * s0 : STRIP * s0 + T].bitcast(FP8X4),
                rhs_scale=x_planes[n][shift][:, plane_col : plane_col + T],
                start=(l == 0),
                stop=(l == N_LAGS - 1),
            )

        def multiply(r):
            for n in range(BATCHES):
                for l in range(first_lag[r], first_lag[r] + ROUNDS[r]):
                    mx_pass(l, n)

        out_t = {}

        def evacuate(n):
            o_t = keep.tile([P, T], F32, name="out_t%d" % n)
            nc.vector.tensor_scalar_add(
                out=o_t[:].rearrange("p (c w) -> p c w", w=WINDOW),
                in0=acc[n][:].rearrange("p (w c) -> p c w", c=STRIP),
                scalar1=bias[:, 0:1],
            )
            out_t[n] = o_t

        def finish(n):
            for pair in range(2):
                unit = out_unit + 2 * n + pair
                tp = bank(unit, [P, 2 * BANK_LAGS, P])
                for j in range(2):
                    t0 = (2 * pair + j) * P
                    nc.tensor.transpose(tp[:, j, :], out_t[n][:, t0 : t0 + P], ident[:])
                res = keep.tile([P, 2, O], F32, name="res%d_%d" % (n, pair))
                if pair == 0:
                    nc.scalar.copy(out=res[:], in_=tp[:, 0:2, :])
                else:
                    nc.vector.tensor_copy(out=res[:], in_=tp[:, 0:2, :])
                nc.sync.dma_start(
                    out=out[n, 2 * pair * P : (2 * pair + 2) * P, :].rearrange("(j p) o -> p j o", p=P),
                    in_=res[:],
                )

        upper_strips(0)
        upper_planes(0)
        transpose_w(0)
        keep_clock(1)
        upper_strips(1)
        quantise_w(0)
        upper_planes(1)
        prepare(1)
        keep_clock(1)
        prepare(2)
        keep_clock(1)
        multiply(0)
        lower_strips(0)
        lower_strips(1)
        nc.vector.tensor_copy(out=bias_row_f32[:], in_=bias_row[:])
        prepare(3)
        multiply(1)
        multiply(2)
        prepare(4)
        multiply(3)
        prepare(5)
        multiply(4)
        prepare(6)

        tail = list(range(first_lag[n_rounds - TAIL_ROUNDS], N_LAGS))
        for l in tail:
            mx_pass(l, 0)
        evacuate(0)
        for l in tail[:HOLD]:
            mx_pass(l, 1)
        finish(0)
        for l in tail[HOLD:]:
            mx_pass(l, 1)
        evacuate(1)
        finish(1)
